import numpy as np
import ml_dtypes


def mxq(x, axis, fmt="e4m3"):
    dtype, down = {"e4m3": (ml_dtypes.float8_e4m3fn, 7), "e5m2": (ml_dtypes.float8_e5m2, 14)}[fmt]
    v = np.moveaxis(np.asarray(x, np.float32).astype(ml_dtypes.bfloat16).astype(np.float64), axis, -1)
    blocks = v.reshape(v.shape[:-1] + (-1, 32))
    amax = np.abs(blocks).max(-1, keepdims=True)
    byte = np.maximum(np.where(amax > 0, np.frexp(amax)[1] - 1 + 127, 0) - down, 1)
    scale = np.exp2(byte - 127.0)
    codes = (blocks / scale).astype(np.float32).astype(dtype).astype(np.float64)
    return np.moveaxis((codes * scale).reshape(v.shape), -1, axis)


WIDE = False


def mx_kscale(k):
    if not WIDE:
        return np.ones(k)
    levels = np.array([10, -10, 5, -5, 0])
    a = np.random.permutation(np.resize(levels, k // 512 * 4)).reshape(k // 512, 4)
    idx = np.arange(k)
    return np.exp2(a[idx // 512, idx % 128 // 32])


BF16 = ml_dtypes.bfloat16


def bf(x):
    return np.asarray(x, np.float32).astype(BF16)


def f64(x):
    return np.asarray(x).astype(np.float64)


E2M1 = np.array([0.0, 0.5, 1.0, 1.5, 2.0, 3.0, 4.0, 6.0, -0.0, -0.5, -1.0, -1.5, -2.0, -3.0, -4.0, -6.0])


def pack_weight(w, fmt):
    k, n = w.shape
    w = f64(bf(w)).reshape(k // 32, 32, n)
    amax = np.abs(w).max(1)
    if fmt == "e4m3":
        byte = np.frexp(amax)[1] - 1 + 127 - 7
    else:
        mant, ex = np.frexp(amax / 6.0)
        byte = np.where(mant > 0.5, ex, ex - 1) + 127
    byte = np.clip(np.where(amax > 0, byte, 1), 1, 254)
    scaled = (w * np.exp2(127.0 - byte)[:, None, :]).reshape(k, n).astype(np.float32)
    by_word = np.ascontiguousarray(scaled.reshape(k // 512, 128, 4, n).transpose(0, 1, 3, 2))
    if fmt == "e4m3":
        words = by_word.astype(ml_dtypes.float8_e4m3fn).view(np.uint8)
    else:
        c = by_word.astype(ml_dtypes.float4_e2m1fn).view(np.uint8) & 0xF
        words = c[..., 0::2] | (c[..., 1::2] << 4)
    return np.ascontiguousarray(words), np.ascontiguousarray(byte.astype(np.uint8).reshape(k // 512, 16, n))


def unpack_weight(words, scales, fmt):
    g, p, n, _ = words.shape
    if fmt == "e4m3":
        vals = np.ascontiguousarray(words).view(ml_dtypes.float8_e4m3fn).astype(np.float64)
    else:
        nib = np.empty((g, p, n, 4), np.uint8)
        nib[..., 0::2] = words & 0xF
        nib[..., 1::2] = words >> 4
        vals = E2M1[nib]
    vals = vals * np.repeat(np.exp2(scales.astype(np.float64) - 127.0), 8, axis=1)[..., None]
    return vals.transpose(0, 1, 3, 2).reshape(g * 512, n)

def pack4(w):
    words, scales = pack_weight(w, "e2m1")
    return words.reshape(words.shape[0], 128, -1), scales


def unpack4(words, scales):
    return unpack_weight(words.reshape(words.shape[0], 128, -1, 2), scales, "e2m1")


B, F, H, C = 512, 1024, 128, 10
EPS = 4.0 / 30.0
P_KEEP = 0.95


def setup_inputs():
    s = mx_kscale(F)
    ns = EPS / (6.0 * np.sqrt(H))
    x1 = bf(np.random.standard_normal((B, F)) * s)
    x2 = bf(np.random.standard_normal((B, F)) * s)
    W1_words, W1_scales = pack4(np.random.standard_normal((F, H)) / np.sqrt(F) / s[:, None])
    b1 = bf(np.random.standard_normal(H) * 0.3)
    W2_words, W2_scales = pack4(np.random.standard_normal((F, H)) / np.sqrt(F) / s[:, None])
    b2 = bf(np.random.standard_normal(H) * 0.3)
    noise_std = bf(np.random.laplace(size=(B, H)) * ns)
    rr_uniform = bf(np.random.uniform(size=H))
    return {"x1": x1,
            "x2": x2,
            "W1_words": W1_words,
            "W1_scales": W1_scales,
            "b1": b1,
            "W2_words": W2_words,
            "W2_scales": W2_scales,
            "b2": b2,
            "noise_std": noise_std,
            "rr_uniform": rr_uniform}


def reference(x1, x2, W1_words, W1_scales, b1, W2_words, W2_scales, b2, noise_std, rr_uniform):
    out1 = (mxq(f64(x1), 1, "e4m3") @ unpack4(W1_words, W1_scales)) + f64(b1)
    one_norm = np.sum(np.abs(out1), axis=1)
    sensitivity = np.max(one_norm) - np.min(one_norm)
    noise_mul = sensitivity / EPS
    out1 = out1 + f64(noise_std) * noise_mul
    rr_mask = np.where(f64(rr_uniform) < P_KEEP, 1.0, 0.0)
    out1 = out1 * rr_mask
    out2 = (mxq(f64(x2), 1, "e4m3") @ unpack4(W2_words, W2_scales)) + f64(b2)
    return np.minimum(out1, out2)

@@ -1,0 +1,245 @@
+from contextlib import ExitStack
+
+import concourse.mybir as mybir
+from concourse.masks import make_identity
+
+F32 = mybir.dt.float32
+BF16 = mybir.dt.bfloat16
+I32 = mybir.dt.int32
+U32 = mybir.dt.uint32
+U8 = mybir.dt.uint8
+FP8X4 = mybir.dt.float8_e4m3fn_x4
+FP4X4 = mybir.dt.float4_e2m1fn_x4
+ALU = mybir.AluOpType
+ACT = mybir.ActivationFunctionType
+AX = mybir.AxisListType
+
+P = 128
+PACK = 4
+K_PASS = P * PACK
+PAIRS = PACK // 2
+B, F, H = 512, 1024, 128
+J = B // P
+G = F // K_PASS
+LAST = J - 1
+EPS = 4.0 / 30.0
+P_KEEP = 0.95
+
+UNITS = [(j, 0, G) for j in range(LAST)] + [(LAST, g, g + 1) for g in range(G)]
+UNITS1 = [(0, g, g + 1) for g in range(G)] + UNITS[1:]
+
+FLOPS = 2 * 2 * B * F * H
+
+
+def tile_splitnn_pa_s_kernel(
+    tc, x1, x2, W1_words, W1_scales, b1, W2_words, W2_scales, b2, noise_std, rr_uniform, out
+):
+    nc = tc.nc
+    x_dram = [x.rearrange("(p j) k -> p j k", j=J) for x in (x1, x2)]
+    words_dram = (W1_words, W2_words)
+    scales_dram = (W1_scales, W2_scales)
+    out_dram = out.rearrange("(p j) h -> p j h", j=J)
+
+    with ExitStack() as stack:
+        const = stack.enter_context(tc.tile_pool(name="const", bufs=1))
+        stage = stack.enter_context(tc.tile_pool(name="stage", bufs=4))
+        xt_pool = stack.enter_context(tc.psum_pool(name="xt_pool", bufs=4))
+        acc_pool = stack.enter_context(tc.psum_pool(name="acc_pool", bufs=4))
+        stack.enter_context(tc.manual_schedule())
+
+        x_sb0 = const.tile([P, J, F], BF16)
+        x_sb1 = const.tile([P, J, F], BF16)
+        x_sb = (x_sb0, x_sb1)
+        w_words = const.tile([P, 2, G, 2 * H], U8, align_bytes=64)
+        w_planes = const.tile([P, 2, G, H], U8, align_bytes=64)
+        x_codes = const.tile([P, 2, J, G * P], U32, align_bytes=64)
+        x_planes = const.tile([P, 2, J, G * P], U8, align_bytes=64)
+        ident = const.tile([P, P], F32)
+        ones = const.tile([P, P], BF16)
+        vec_rows = const.tile([P, 3, H], BF16)
+        b1_bc = const.tile([P, H], F32)
+        b2_bc = const.tile([P, H], F32)
+        keep_bc = const.tile([P, H], BF16)
+        noise_sb = const.tile([P, J, H], BF16)
+        noise_kept = const.tile([P, J, H], BF16)
+        a_sb = const.tile([P, J, H], F32)
+        a_kept = const.tile([P, J, H], F32)
+        abs_sb = const.tile([P, J, H], F32)
+        row_norm = const.tile([P, J], F32)
+        tile_ext = const.tile([P, 2], F32)
+        all_ext = const.tile([P, 2], F32)
+        noise_mul = const.tile([P, 1], F32)
+        c_sb = const.tile([P, J, H], F32)
+        d_sb = const.tile([P, J, H], F32)
+        out_sb = const.tile([P, J, H], F32)
+        warm_in = const.tile([P, 1], F32)
+        warm_out = const.tile([P, 1], F32)
+
+        nc.vector.memset(vec_rows[:], 0.0)
+        nc.vector.memset(ones[:], 1.0)
+        nc.vector.memset(w_planes[:].rearrange("p c g h -> p (c g h)").bitcast(I32), 0)
+        nc.vector.memset(warm_in[:], 0.0)
+        make_identity(nc, ident[:])
+        nc.scalar.activation(out=warm_out[:], in_=warm_in[:], func=ACT.Abs)
+
+        def load_x(c, j0, j1):
+            nc.sync.dma_start(out=x_sb[c][:, j0:j1, :], in_=x_dram[c][:, j0:j1, :])
+
+        def load_vector(i, vec):
+            nc.sync.dma_start(out=vec_rows[0:1, i, :], in_=vec.rearrange("(o h) -> o h", o=1))
+
+        def load_weight(c):
+            nc.sync.dma_start(
+                out=w_words[:, c, :, :].bitcast(I32),
+                in_=words_dram[c].bitcast(I32).rearrange("g p n -> p g n"),
+            )
+            for quad in range(4):
+                nc.sync.dma_start(
+                    out=w_planes[32 * quad : 32 * quad + 4, c, :, :].bitcast(I32),
+                    in_=scales_dram[c].bitcast(I32)[:, 4 * quad : 4 * quad + 4, :].rearrange("g r n -> r g n"),
+                )
+
+        for g in range(G):
+            k_cols = slice(g * K_PASS, (g + 1) * K_PASS)
+            nc.sync.dma_start(out=x_sb[0][:, 0, k_cols], in_=x_dram[0][:, 0, k_cols])
+        load_vector(0, b1)
+        for j in range(1, J):
+            load_x(0, j, j + 1)
+        load_x(1, 0, 1)
+        load_weight(0)
+        load_x(1, 1, 2)
+        load_x(1, 2, J)
+        load_weight(1)
+        nc.sync.dma_start(out=noise_sb[:], in_=noise_std.rearrange("(p j) h -> p j h", j=J))
+        nc.gpsimd.dma_start(out=vec_rows[0:1, 1, :], in_=rr_uniform.rearrange("(o h) -> o h", o=1))
+        nc.gpsimd.dma_start(out=vec_rows[0:1, 2, :], in_=b2.rearrange("(o h) -> o h", o=1))
+
+        grouped_of = {}
+
+        def transpose_unit(c, unit):
+            j, g0, g1 = unit
+            n_pass = g1 - g0
+            x_words = x_sb[c][:, j, :].bitcast(F32)
+            xt = xt_pool.tile([P, n_pass * PAIRS, P], F32, tag="xt")
+            for g in range(g0, g1):
+                for u in range(PAIRS):
+                    nc.tensor.transpose(
+                        xt[:, PAIRS * (g - g0) + u, :],
+                        x_words[:, 256 * g + u : 256 * (g + 1) : PAIRS],
+                        ident[:],
+                    )
+            grouped = stage.tile([P, n_pass * P * PACK], BF16, align_bytes=64, tag="grouped")
+            nc.scalar.copy(
+                out=grouped[:].bitcast(F32).rearrange("p (g b u) -> p g b u", g=n_pass, u=PAIRS),
+                in_=xt[:].rearrange("p (g u) b -> p g b u", u=PAIRS),
+            )
+            grouped_of[(c, unit)] = grouped
+
+        def quantise_unit(c, unit):
+            j, g0, g1 = unit
+            cols = slice(g0 * P, g1 * P)
+            nc.vector.quantize_mx(
+                out=x_codes[:, c, j, cols].bitcast(FP8X4),
+                scales=x_planes[:, c, j, cols],
+                in_=grouped_of[(c, unit)][:],
+            )
+
+        def project_tile(c, j, acc):
+            for g in range(G):
+                cols = slice(g * P, (g + 1) * P)
+                nc.tensor.matmul_mx(
+                    out=acc,
+                    lhsT=x_codes[:, c, j, cols].bitcast(FP8X4),
+                    lhsT_scale=x_planes[:, c, j, cols],
+                    rhs=w_words[:, c, g, :].bitcast(FP4X4),
+                    rhs_scale=w_planes[:, c, g, :],
+                    start=(g == 0),
+                    stop=(g == G - 1),
+                )
+
+        def spread_vector(i):
+            vec_ps = xt_pool.tile([P, H], F32, tag="xt")
+            nc.tensor.matmul(out=vec_ps[:], lhsT=ones[:], rhs=vec_rows[:, i, :], start=True, stop=True)
+            return vec_ps
+
+        def noisy_rows(j0, j1):
+            nc.vector.scalar_tensor_tensor(
+                out=c_sb[:, j0:j1, :].rearrange("p j h -> p (j h)"),
+                in0=noise_kept[:, j0:j1, :].rearrange("p j h -> p (j h)"),
+                scalar=noise_mul[:, 0:1],
+                in1=a_kept[:, j0:j1, :].rearrange("p j h -> p (j h)"),
+                op0=ALU.mult,
+                op1=ALU.add,
+            )
+
+        def client2_rows(j0, j1):
+            acc = acc_pool.tile([P, j1 - j0, H], F32, tag="acc")
+            for j in range(j0, j1):
+                project_tile(1, j, acc[:, j - j0, :])
+            b2_rows = b2_bc[:].unsqueeze(1).to_broadcast([P, j1 - j0, H])
+            nc.vector.tensor_tensor(out=d_sb[:, j0:j1, :], in0=acc[:], in1=b2_rows, op=ALU.add)
+
+        def finish_rows(j0, j1):
+            nc.vector.tensor_tensor(
+                out=out_sb[:, j0:j1, :], in0=c_sb[:, j0:j1, :], in1=d_sb[:, j0:j1, :], op=ALU.min
+            )
+            nc.sync.dma_start(out=out_dram[:, j0:j1, :], in_=out_sb[:, j0:j1, :])
+
+
+        transpose_unit(0, UNITS1[0])
+        transpose_unit(0, UNITS1[1])
+        b1_ps = spread_vector(0)
+        nc.scalar.copy(out=b1_bc[:], in_=b1_ps[:])
+        for unit in UNITS1[2:]:
+            transpose_unit(0, unit)
+        transpose_unit(1, UNITS[0])
+        for unit in UNITS1:
+            quantise_unit(0, unit)
+
+        for j in range(J):
+            acc = acc_pool.tile([P, H], F32, tag="acc")
+            project_tile(0, j, acc[:])
+            nc.vector.tensor_tensor(out=a_sb[:, j, :], in0=acc[:], in1=b1_bc[:], op=ALU.add)
+            nc.scalar.activation(
+                out=abs_sb[:, j, :], in_=a_sb[:, j, :], func=ACT.Abs, accum_out=row_norm[:, j : j + 1]
+            )
+        rr_ps = spread_vector(1)
+        b2_ps = spread_vector(2)
+        nc.scalar.copy(out=b2_bc[:], in_=b2_ps[:])
+
+        quantise_unit(1, UNITS[0])
+        nc.vector.tensor_single_scalar(out=keep_bc[:], in_=rr_ps[:], scalar=P_KEEP, op=ALU.is_lt)
+        keep_all = keep_bc[:].unsqueeze(1).to_broadcast([P, J, H])
+        nc.vector.tensor_reduce(out=tile_ext[:, 0:1], in_=row_norm[:], axis=AX.X, op=ALU.max)
+        nc.vector.tensor_reduce(out=tile_ext[:, 1:2], in_=row_norm[:], axis=AX.X, op=ALU.min, negate=True)
+        nc.vector.tensor_tensor(out=a_kept[:], in0=a_sb[:], in1=keep_all, op=ALU.mult)
+        transpose_unit(1, UNITS[1])
+        transpose_unit(1, UNITS[2])
+        quantise_unit(1, UNITS[1])
+        ext_ps = acc_pool.tile([P, 2, P], F32, tag="acc")
+        for i in range(2):
+            nc.tensor.transpose(ext_ps[:, i, :], tile_ext[:, i : i + 1].to_broadcast([P, P]), ident[:])
+        nc.vector.tensor_reduce(out=all_ext[:], in_=ext_ps[:], axis=AX.X, op=ALU.max)
+        transpose_unit(1, UNITS[3])
+        transpose_unit(1, UNITS[4])
+        nc.vector.tensor_tensor(out=noise_kept[:], in0=noise_sb[:], in1=keep_all, op=ALU.mult)
+        nc.vector.tensor_scalar(
+            out=noise_mul[:],
+            in0=all_ext[:, 0:1],
+            scalar1=all_ext[:, 1:2],
+            scalar2=1.0 / EPS,
+            op0=ALU.add,
+            op1=ALU.mult,
+        )
+        quantise_unit(1, UNITS[2])
+        noisy_rows(0, 2)
+        quantise_unit(1, UNITS[3])
+        noisy_rows(2, J)
+        quantise_unit(1, UNITS[4])
+
+        client2_rows(0, 2)
+        client2_rows(2, LAST)
+        finish_rows(0, 2)
+        client2_rows(LAST, J)
+        finish_rows(2, LAST)
+        finish_rows(LAST, J)

@@ -26,7 +26,11 @@ EPS = 4.0 / 30.0
 P_KEEP = 0.95
 
 UNITS = [(j, 0, G) for j in range(LAST)] + [(LAST, g, g + 1) for g in range(G)]
-UNITS1 = [(0, g, g + 1) for g in range(G)] + UNITS[1:]
+UNITS1 = [(j, g, g + 1) for j in range(J) for g in range(G)]
+
+WARM = 3
+
+LAST_T = 3
 
 FLOPS = 2 * 2 * B * F * H
 
@@ -42,7 +46,7 @@ def tile_splitnn_pa_s_kernel(
 
     with ExitStack() as stack:
         const = stack.enter_context(tc.tile_pool(name="const", bufs=1))
-        stage = stack.enter_context(tc.tile_pool(name="stage", bufs=4))
+        stage = stack.enter_context(tc.tile_pool(name="stage", bufs=6))
         xt_pool = stack.enter_context(tc.psum_pool(name="xt_pool", bufs=4))
         acc_pool = stack.enter_context(tc.psum_pool(name="acc_pool", bufs=4))
         stack.enter_context(tc.manual_schedule())
@@ -58,6 +62,8 @@ def tile_splitnn_pa_s_kernel(
         ones = const.tile([P, P], BF16)
         vec_rows = const.tile([P, 3, H], BF16)
         b1_bc = const.tile([P, H], F32)
+        b2_col = const.tile([P, 1], F32)
+        d_t = const.tile([P, J, P], F32)
         b2_bc = const.tile([P, H], F32)
         keep_bc = const.tile([P, H], BF16)
         noise_sb = const.tile([P, J, H], BF16)
@@ -102,19 +108,20 @@ def tile_splitnn_pa_s_kernel(
         for g in range(G):
             k_cols = slice(g * K_PASS, (g + 1) * K_PASS)
             nc.sync.dma_start(out=x_sb[0][:, 0, k_cols], in_=x_dram[0][:, 0, k_cols])
+        load_x(0, 1, 2)
         load_vector(0, b1)
-        for j in range(1, J):
-            load_x(0, j, j + 1)
+        load_vector(1, rr_uniform)
+        load_vector(2, b2)
+        load_x(0, 2, 3)
+        load_x(0, 3, 4)
         load_x(1, 0, 1)
         load_weight(0)
         load_x(1, 1, 2)
-        load_x(1, 2, J)
+        load_x(1, 2, 4)
         load_weight(1)
-        nc.sync.dma_start(out=noise_sb[:], in_=noise_std.rearrange("(p j) h -> p j h", j=J))
-        nc.gpsimd.dma_start(out=vec_rows[0:1, 1, :], in_=rr_uniform.rearrange("(o h) -> o h", o=1))
-        nc.gpsimd.dma_start(out=vec_rows[0:1, 2, :], in_=b2.rearrange("(o h) -> o h", o=1))
+        nc.gpsimd.dma_start(out=noise_sb[:], in_=noise_std.rearrange("(p j) h -> p j h", j=J))
 
-        grouped_of = {}
+        xt_of, grouped_of, d_of, acc_of = {}, {}, {}, {}
 
         def transpose_unit(c, unit):
             j, g0, g1 = unit
@@ -128,10 +135,15 @@ def tile_splitnn_pa_s_kernel(
                         x_words[:, 256 * g + u : 256 * (g + 1) : PAIRS],
                         ident[:],
                     )
+            xt_of[(c, unit)] = xt
+
+        def regroup_unit(c, unit, copy):
+            j, g0, g1 = unit
+            n_pass = g1 - g0
             grouped = stage.tile([P, n_pass * P * PACK], BF16, align_bytes=64, tag="grouped")
-            nc.scalar.copy(
+            copy(
                 out=grouped[:].bitcast(F32).rearrange("p (g b u) -> p g b u", g=n_pass, u=PAIRS),
-                in_=xt[:].rearrange("p (g u) b -> p g b u", u=PAIRS),
+                in_=xt_of[(c, unit)][:].rearrange("p (g u) b -> p g b u", u=PAIRS),
             )
             grouped_of[(c, unit)] = grouped
 
@@ -144,23 +156,21 @@ def tile_splitnn_pa_s_kernel(
                 in_=grouped_of[(c, unit)][:],
             )
 
-        def project_tile(c, j, acc):
+        def project_tile(c, j, acc, transposed=False):
             for g in range(G):
                 cols = slice(g * P, (g + 1) * P)
+                x_side = (x_codes[:, c, j, cols].bitcast(FP8X4), x_planes[:, c, j, cols])
+                w_side = (w_words[:, c, g, :].bitcast(FP4X4), w_planes[:, c, g, :])
+                lhs, rhs = (w_side, x_side) if transposed else (x_side, w_side)
                 nc.tensor.matmul_mx(
                     out=acc,
-                    lhsT=x_codes[:, c, j, cols].bitcast(FP8X4),
-                    lhsT_scale=x_planes[:, c, j, cols],
-                    rhs=w_words[:, c, g, :].bitcast(FP4X4),
-                    rhs_scale=w_planes[:, c, g, :],
+                    lhsT=lhs[0],
+                    lhsT_scale=lhs[1],
+                    rhs=rhs[0],
+                    rhs_scale=rhs[1],
                     start=(g == 0),
                     stop=(g == G - 1),
                 )
-
-        def spread_vector(i):
-            vec_ps = xt_pool.tile([P, H], F32, tag="xt")
-            nc.tensor.matmul(out=vec_ps[:], lhsT=ones[:], rhs=vec_rows[:, i, :], start=True, stop=True)
-            return vec_ps
 
         def noisy_rows(j0, j1):
             nc.vector.scalar_tensor_tensor(
@@ -172,57 +182,123 @@ def tile_splitnn_pa_s_kernel(
                 op1=ALU.add,
             )
 
-        def client2_rows(j0, j1):
+        def client2_mx(j0, j1):
             acc = acc_pool.tile([P, j1 - j0, H], F32, tag="acc")
             for j in range(j0, j1):
                 project_tile(1, j, acc[:, j - j0, :])
+            acc_of[j0] = acc
+
+        def client2_add(j0, j1):
             b2_rows = b2_bc[:].unsqueeze(1).to_broadcast([P, j1 - j0, H])
-            nc.vector.tensor_tensor(out=d_sb[:, j0:j1, :], in0=acc[:], in1=b2_rows, op=ALU.add)
+            nc.vector.tensor_tensor(out=d_sb[:, j0:j1, :], in0=acc_of[j0][:], in1=b2_rows, op=ALU.add)
+
+        def client2_product(j0, j1):
+            acc = acc_pool.tile([P, j1 - j0, P], F32, tag="acc")
+            for j in range(j0, j1):
+                project_tile(1, j, acc[:, j - j0, :], transposed=True)
+            nc.scalar.activation(out=d_t[:, j0:j1, :], in_=acc[:], func=ACT.Identity, bias=b2_col[:, 0:1])
+
+        def client2_back(j0, j1):
+            d_ps = xt_pool.tile([P, j1 - j0, H], F32, tag="xt")
+            for j in range(j0, j1):
+                nc.tensor.transpose(d_ps[:, j - j0, :], d_t[:, j, :], ident[:])
+            d_of[j0] = d_ps
 
         def finish_rows(j0, j1):
-            nc.vector.tensor_tensor(
-                out=out_sb[:, j0:j1, :], in0=c_sb[:, j0:j1, :], in1=d_sb[:, j0:j1, :], op=ALU.min
-            )
+            d = d_of[j0] if j0 in d_of else None
+            in1 = d_sb[:, j0:j1, :] if d is None or j0 >= LAST_T else d[:]
+            nc.vector.tensor_tensor(out=out_sb[:, j0:j1, :], in0=c_sb[:, j0:j1, :], in1=in1, op=ALU.min)
             nc.sync.dma_start(out=out_dram[:, j0:j1, :], in_=out_sb[:, j0:j1, :])
 
-
+        warm_ps = acc_pool.tile([P, WARM, P], F32, tag="acc")
+        for i in range(WARM):
+            nc.tensor.matmul(out=warm_ps[:, i, :], lhsT=ident[:], rhs=ident[:], start=True, stop=True)
         transpose_unit(0, UNITS1[0])
+        regroup_unit(0, UNITS1[0], nc.scalar.copy)
         transpose_unit(0, UNITS1[1])
-        b1_ps = spread_vector(0)
-        nc.scalar.copy(out=b1_bc[:], in_=b1_ps[:])
-        for unit in UNITS1[2:]:
-            transpose_unit(0, unit)
-        transpose_unit(1, UNITS[0])
-        for unit in UNITS1:
-            quantise_unit(0, unit)
-
-        for j in range(J):
-            acc = acc_pool.tile([P, H], F32, tag="acc")
-            project_tile(0, j, acc[:])
-            nc.vector.tensor_tensor(out=a_sb[:, j, :], in0=acc[:], in1=b1_bc[:], op=ALU.add)
-            nc.scalar.activation(
-                out=abs_sb[:, j, :], in_=a_sb[:, j, :], func=ACT.Abs, accum_out=row_norm[:, j : j + 1]
-            )
-        rr_ps = spread_vector(1)
-        b2_ps = spread_vector(2)
-        nc.scalar.copy(out=b2_bc[:], in_=b2_ps[:])
-
-        quantise_unit(1, UNITS[0])
-        nc.vector.tensor_single_scalar(out=keep_bc[:], in_=rr_ps[:], scalar=P_KEEP, op=ALU.is_lt)
+        regroup_unit(0, UNITS1[1], nc.scalar.copy)
+        quantise_unit(0, UNITS1[0])
+        transpose_unit(0, UNITS1[2])
+        regroup_unit(0, UNITS1[2], nc.scalar.copy)
+        transpose_unit(0, UNITS1[3])
+        quantise_unit(0, UNITS1[1])
+        bc1 = acc_pool.tile([P, 2, H], F32, tag="acc")
+        nc.tensor.matmul(
+            out=bc1[:].rearrange("p v h -> p (v h)"),
+            lhsT=ones[:],
+            rhs=vec_rows[:, 0:2, :].rearrange("p v h -> p (v h)"),
+            start=True,
+            stop=True,
+        )
+        regroup_unit(0, UNITS1[3], nc.scalar.copy)
+        nc.vector.tensor_copy(out=b1_bc[:], in_=bc1[:, 0, :])
+        nc.vector.tensor_single_scalar(out=keep_bc[:], in_=bc1[:, 1, :], scalar=P_KEEP, op=ALU.is_lt)
         keep_all = keep_bc[:].unsqueeze(1).to_broadcast([P, J, H])
+        transpose_unit(0, UNITS1[4])
+        regroup_unit(0, UNITS1[4], nc.scalar.copy)
+        quantise_unit(0, UNITS1[2])
+        transpose_unit(0, UNITS1[5])
+        regroup_unit(0, UNITS1[5], nc.scalar.copy)
+        quantise_unit(0, UNITS1[3])
+        transpose_unit(0, UNITS1[6])
+        regroup_unit(0, UNITS1[6], nc.scalar.copy)
+        quantise_unit(0, UNITS1[4])
+        quantise_unit(0, UNITS1[5])
+        transpose_unit(0, UNITS1[7])
+        regroup_unit(0, UNITS1[7], nc.scalar.copy)
+        bc2 = acc_pool.tile([P, 1, H], F32, tag="acc")
+        nc.tensor.matmul(
+            out=bc2[:].rearrange("p v h -> p (v h)"),
+            lhsT=ones[:],
+            rhs=vec_rows[:, 2:3, :].rearrange("p v h -> p (v h)"),
+            start=True,
+            stop=True,
+        )
+        colb = acc_pool.tile([P, 2], F32, tag="acc")
+        nc.tensor.matmul(out=colb[:], lhsT=vec_rows[:, 2, :], rhs=ones[:, 0:2], start=True, stop=True)
+        nc.vector.tensor_copy(out=b2_bc[:], in_=bc2[:, 0, :])
+        nc.vector.tensor_copy(out=b2_col[:], in_=colb[:, 0:1])
+        quantise_unit(0, UNITS1[6])
+        quantise_unit(0, UNITS1[7])
+        transpose_unit(1, UNITS[0])
+        regroup_unit(1, UNITS[0], nc.scalar.copy)
+        acc1_0 = acc_pool.tile([P, H], F32, tag="acc")
+        project_tile(0, 0, acc1_0[:])
+        acc1_1 = acc_pool.tile([P, H], F32, tag="acc")
+        project_tile(0, 1, acc1_1[:])
+        nc.vector.tensor_tensor(out=a_sb[:, 0, :], in0=acc1_0[:], in1=b1_bc[:], op=ALU.add)
+        nc.vector.tensor_tensor(out=a_sb[:, 1, :], in0=acc1_1[:], in1=b1_bc[:], op=ALU.add)
+        acc1_2 = acc_pool.tile([P, H], F32, tag="acc")
+        project_tile(0, 2, acc1_2[:])
+        acc1_3 = acc_pool.tile([P, H], F32, tag="acc")
+        project_tile(0, 3, acc1_3[:])
+        nc.vector.tensor_tensor(out=a_sb[:, 2, :], in0=acc1_2[:], in1=b1_bc[:], op=ALU.add)
+        nc.vector.tensor_tensor(out=a_kept[:, 0:1, :], in0=a_sb[:, 0:1, :], in1=keep_all[:, 0:1, :], op=ALU.mult)
+        nc.vector.tensor_tensor(out=a_sb[:, 3, :], in0=acc1_3[:], in1=b1_bc[:], op=ALU.add)
+        nc.vector.tensor_tensor(out=a_kept[:, 1:2, :], in0=a_sb[:, 1:2, :], in1=keep_all[:, 1:2, :], op=ALU.mult)
+        nc.scalar.activation(out=abs_sb[:, 0, :], in_=a_sb[:, 0, :], func=ACT.Abs, accum_out=row_norm[:, 0 : 0 + 1])
+        nc.scalar.activation(out=abs_sb[:, 1, :], in_=a_sb[:, 1, :], func=ACT.Abs, accum_out=row_norm[:, 1 : 1 + 1])
+        nc.scalar.activation(out=abs_sb[:, 2, :], in_=a_sb[:, 2, :], func=ACT.Abs, accum_out=row_norm[:, 2 : 2 + 1])
+        nc.scalar.activation(out=abs_sb[:, 3, :], in_=a_sb[:, 3, :], func=ACT.Abs, accum_out=row_norm[:, 3 : 3 + 1])
+        transpose_unit(1, UNITS[1])
+        regroup_unit(1, UNITS[1], nc.scalar.copy)
+        transpose_unit(1, UNITS[2])
+        regroup_unit(1, UNITS[2], nc.scalar.copy)
+        quantise_unit(1, UNITS[0])
+        nc.vector.tensor_tensor(out=noise_kept[:], in0=noise_sb[:], in1=keep_all, op=ALU.mult)
         nc.vector.tensor_reduce(out=tile_ext[:, 0:1], in_=row_norm[:], axis=AX.X, op=ALU.max)
         nc.vector.tensor_reduce(out=tile_ext[:, 1:2], in_=row_norm[:], axis=AX.X, op=ALU.min, negate=True)
-        nc.vector.tensor_tensor(out=a_kept[:], in0=a_sb[:], in1=keep_all, op=ALU.mult)
-        transpose_unit(1, UNITS[1])
-        transpose_unit(1, UNITS[2])
-        quantise_unit(1, UNITS[1])
+        nc.vector.tensor_tensor(out=a_kept[:, 2:4, :], in0=a_sb[:, 2:4, :], in1=keep_all[:, 2:4, :], op=ALU.mult)
+        transpose_unit(1, UNITS[3])
+        regroup_unit(1, UNITS[3], nc.scalar.copy)
+        transpose_unit(1, UNITS[4])
+        regroup_unit(1, UNITS[4], nc.scalar.copy)
         ext_ps = acc_pool.tile([P, 2, P], F32, tag="acc")
         for i in range(2):
             nc.tensor.transpose(ext_ps[:, i, :], tile_ext[:, i : i + 1].to_broadcast([P, P]), ident[:])
+        quantise_unit(1, UNITS[1])
         nc.vector.tensor_reduce(out=all_ext[:], in_=ext_ps[:], axis=AX.X, op=ALU.max)
-        transpose_unit(1, UNITS[3])
-        transpose_unit(1, UNITS[4])
-        nc.vector.tensor_tensor(out=noise_kept[:], in0=noise_sb[:], in1=keep_all, op=ALU.mult)
+        quantise_unit(1, UNITS[2])
         nc.vector.tensor_scalar(
             out=noise_mul[:],
             in0=all_ext[:, 0:1],
@@ -231,15 +307,16 @@ def tile_splitnn_pa_s_kernel(
             op0=ALU.add,
             op1=ALU.mult,
         )
-        quantise_unit(1, UNITS[2])
-        noisy_rows(0, 2)
+        client2_product(0, 2)
         quantise_unit(1, UNITS[3])
-        noisy_rows(2, J)
+        client2_product(2, LAST)
+        noisy_rows(0, 2)
+        client2_back(0, 2)
         quantise_unit(1, UNITS[4])
-
-        client2_rows(0, 2)
-        client2_rows(2, LAST)
+        client2_mx(LAST, J)
+        client2_back(2, LAST)
+        noisy_rows(2, J)
         finish_rows(0, 2)
-        client2_rows(LAST, J)
+        client2_add(LAST, J)
         finish_rows(2, LAST)
         finish_rows(LAST, J)

@@ -28,8 +28,6 @@ P_KEEP = 0.95
 UNITS = [(j, 0, G) for j in range(LAST)] + [(LAST, g, g + 1) for g in range(G)]
 UNITS1 = [(j, g, g + 1) for j in range(J) for g in range(G)]
 
-WARM = 3
-
 LAST_T = 3
 
 FLOPS = 2 * 2 * B * F * H
@@ -118,8 +116,8 @@ def tile_splitnn_pa_s_kernel(
         load_weight(0)
         load_x(1, 1, 2)
         load_x(1, 2, 4)
+        nc.sync.dma_start(out=noise_sb[:], in_=noise_std.rearrange("(p j) h -> p j h", j=J))
         load_weight(1)
-        nc.gpsimd.dma_start(out=noise_sb[:], in_=noise_std.rearrange("(p j) h -> p j h", j=J))
 
         xt_of, grouped_of, d_of, acc_of = {}, {}, {}, {}
 
@@ -210,9 +208,6 @@ def tile_splitnn_pa_s_kernel(
             nc.vector.tensor_tensor(out=out_sb[:, j0:j1, :], in0=c_sb[:, j0:j1, :], in1=in1, op=ALU.min)
             nc.sync.dma_start(out=out_dram[:, j0:j1, :], in_=out_sb[:, j0:j1, :])
 
-        warm_ps = acc_pool.tile([P, WARM, P], F32, tag="acc")
-        for i in range(WARM):
-            nc.tensor.matmul(out=warm_ps[:, i, :], lhsT=ident[:], rhs=ident[:], start=True, stop=True)
         transpose_unit(0, UNITS1[0])
         regroup_unit(0, UNITS1[0], nc.scalar.copy)
         transpose_unit(0, UNITS1[1])

@@ -26,9 +26,9 @@ EPS = 4.0 / 30.0
 P_KEEP = 0.95
 
 UNITS = [(j, 0, G) for j in range(LAST)] + [(LAST, g, g + 1) for g in range(G)]
-UNITS1 = [(j, g, g + 1) for j in range(J) for g in range(G)]
+UNITS1 = [(0, g, g + 1) for g in range(G)] + UNITS[1:]
 
-LAST_T = 3
+LAST_T = 0
 
 FLOPS = 2 * 2 * B * F * H
 
@@ -109,7 +109,6 @@ def tile_splitnn_pa_s_kernel(
         load_x(0, 1, 2)
         load_vector(0, b1)
         load_vector(1, rr_uniform)
-        load_vector(2, b2)
         load_x(0, 2, 3)
         load_x(0, 3, 4)
         load_x(1, 0, 1)
@@ -118,6 +117,8 @@ def tile_splitnn_pa_s_kernel(
         load_x(1, 2, 4)
         nc.sync.dma_start(out=noise_sb[:], in_=noise_std.rearrange("(p j) h -> p j h", j=J))
         load_weight(1)
+
+        nc.gpsimd.dma_start(out=vec_rows[0:1, 2, :], in_=b2.rearrange("(o h) -> o h", o=1))
 
         xt_of, grouped_of, d_of, acc_of = {}, {}, {}, {}
 
@@ -215,7 +216,6 @@ def tile_splitnn_pa_s_kernel(
         quantise_unit(0, UNITS1[0])
         transpose_unit(0, UNITS1[2])
         regroup_unit(0, UNITS1[2], nc.scalar.copy)
-        transpose_unit(0, UNITS1[3])
         quantise_unit(0, UNITS1[1])
         bc1 = acc_pool.tile([P, 2, H], F32, tag="acc")
         nc.tensor.matmul(
@@ -225,36 +225,19 @@ def tile_splitnn_pa_s_kernel(
             start=True,
             stop=True,
         )
-        regroup_unit(0, UNITS1[3], nc.scalar.copy)
         nc.vector.tensor_copy(out=b1_bc[:], in_=bc1[:, 0, :])
         nc.vector.tensor_single_scalar(out=keep_bc[:], in_=bc1[:, 1, :], scalar=P_KEEP, op=ALU.is_lt)
         keep_all = keep_bc[:].unsqueeze(1).to_broadcast([P, J, H])
+        transpose_unit(0, UNITS1[3])
+        regroup_unit(0, UNITS1[3], nc.scalar.copy)
+        quantise_unit(0, UNITS1[2])
         transpose_unit(0, UNITS1[4])
         regroup_unit(0, UNITS1[4], nc.scalar.copy)
-        quantise_unit(0, UNITS1[2])
+        quantise_unit(0, UNITS1[3])
         transpose_unit(0, UNITS1[5])
         regroup_unit(0, UNITS1[5], nc.scalar.copy)
-        quantise_unit(0, UNITS1[3])
-        transpose_unit(0, UNITS1[6])
-        regroup_unit(0, UNITS1[6], nc.scalar.copy)
         quantise_unit(0, UNITS1[4])
         quantise_unit(0, UNITS1[5])
-        transpose_unit(0, UNITS1[7])
-        regroup_unit(0, UNITS1[7], nc.scalar.copy)
-        bc2 = acc_pool.tile([P, 1, H], F32, tag="acc")
-        nc.tensor.matmul(
-            out=bc2[:].rearrange("p v h -> p (v h)"),
-            lhsT=ones[:],
-            rhs=vec_rows[:, 2:3, :].rearrange("p v h -> p (v h)"),
-            start=True,
-            stop=True,
-        )
-        colb = acc_pool.tile([P, 2], F32, tag="acc")
-        nc.tensor.matmul(out=colb[:], lhsT=vec_rows[:, 2, :], rhs=ones[:, 0:2], start=True, stop=True)
-        nc.vector.tensor_copy(out=b2_bc[:], in_=bc2[:, 0, :])
-        nc.vector.tensor_copy(out=b2_col[:], in_=colb[:, 0:1])
-        quantise_unit(0, UNITS1[6])
-        quantise_unit(0, UNITS1[7])
         transpose_unit(1, UNITS[0])
         regroup_unit(1, UNITS[0], nc.scalar.copy)
         acc1_0 = acc_pool.tile([P, H], F32, tag="acc")
@@ -268,13 +251,20 @@ def tile_splitnn_pa_s_kernel(
         acc1_3 = acc_pool.tile([P, H], F32, tag="acc")
         project_tile(0, 3, acc1_3[:])
         nc.vector.tensor_tensor(out=a_sb[:, 2, :], in0=acc1_2[:], in1=b1_bc[:], op=ALU.add)
-        nc.vector.tensor_tensor(out=a_kept[:, 0:1, :], in0=a_sb[:, 0:1, :], in1=keep_all[:, 0:1, :], op=ALU.mult)
         nc.vector.tensor_tensor(out=a_sb[:, 3, :], in0=acc1_3[:], in1=b1_bc[:], op=ALU.add)
-        nc.vector.tensor_tensor(out=a_kept[:, 1:2, :], in0=a_sb[:, 1:2, :], in1=keep_all[:, 1:2, :], op=ALU.mult)
         nc.scalar.activation(out=abs_sb[:, 0, :], in_=a_sb[:, 0, :], func=ACT.Abs, accum_out=row_norm[:, 0 : 0 + 1])
         nc.scalar.activation(out=abs_sb[:, 1, :], in_=a_sb[:, 1, :], func=ACT.Abs, accum_out=row_norm[:, 1 : 1 + 1])
         nc.scalar.activation(out=abs_sb[:, 2, :], in_=a_sb[:, 2, :], func=ACT.Abs, accum_out=row_norm[:, 2 : 2 + 1])
         nc.scalar.activation(out=abs_sb[:, 3, :], in_=a_sb[:, 3, :], func=ACT.Abs, accum_out=row_norm[:, 3 : 3 + 1])
+        bc2 = acc_pool.tile([P, 1, H], F32, tag="acc")
+        nc.tensor.matmul(
+            out=bc2[:].rearrange("p v h -> p (v h)"),
+            lhsT=ones[:],
+            rhs=vec_rows[:, 2:3, :].rearrange("p v h -> p (v h)"),
+            start=True,
+            stop=True,
+        )
+        nc.scalar.copy(out=b2_bc[:], in_=bc2[:, 0, :])
         transpose_unit(1, UNITS[1])
         regroup_unit(1, UNITS[1], nc.scalar.copy)
         transpose_unit(1, UNITS[2])
@@ -283,14 +273,14 @@ def tile_splitnn_pa_s_kernel(
         nc.vector.tensor_tensor(out=noise_kept[:], in0=noise_sb[:], in1=keep_all, op=ALU.mult)
         nc.vector.tensor_reduce(out=tile_ext[:, 0:1], in_=row_norm[:], axis=AX.X, op=ALU.max)
         nc.vector.tensor_reduce(out=tile_ext[:, 1:2], in_=row_norm[:], axis=AX.X, op=ALU.min, negate=True)
-        nc.vector.tensor_tensor(out=a_kept[:, 2:4, :], in0=a_sb[:, 2:4, :], in1=keep_all[:, 2:4, :], op=ALU.mult)
+        nc.vector.tensor_tensor(out=a_kept[:, 0:4, :], in0=a_sb[:, 0:4, :], in1=keep_all[:, 0:4, :], op=ALU.mult)
+        ext_ps = acc_pool.tile([P, 2, P], F32, tag="acc")
+        for i in range(2):
+            nc.tensor.transpose(ext_ps[:, i, :], tile_ext[:, i : i + 1].to_broadcast([P, P]), ident[:])
         transpose_unit(1, UNITS[3])
         regroup_unit(1, UNITS[3], nc.scalar.copy)
         transpose_unit(1, UNITS[4])
         regroup_unit(1, UNITS[4], nc.scalar.copy)
-        ext_ps = acc_pool.tile([P, 2, P], F32, tag="acc")
-        for i in range(2):
-            nc.tensor.transpose(ext_ps[:, i, :], tile_ext[:, i : i + 1].to_broadcast([P, P]), ident[:])
         quantise_unit(1, UNITS[1])
         nc.vector.tensor_reduce(out=all_ext[:], in_=ext_ps[:], axis=AX.X, op=ALU.max)
         quantise_unit(1, UNITS[2])
@@ -302,15 +292,15 @@ def tile_splitnn_pa_s_kernel(
             op0=ALU.add,
             op1=ALU.mult,
         )
-        client2_product(0, 2)
+        client2_mx(0, 2)
         quantise_unit(1, UNITS[3])
-        client2_product(2, LAST)
+        client2_add(0, 2)
         noisy_rows(0, 2)
-        client2_back(0, 2)
+        client2_mx(2, LAST)
         quantise_unit(1, UNITS[4])
-        client2_mx(LAST, J)
-        client2_back(2, LAST)
         noisy_rows(2, J)
+        client2_mx(LAST, J)
+        client2_add(2, LAST)
         finish_rows(0, 2)
         client2_add(LAST, J)
         finish_rows(2, LAST)

@@ -117,7 +117,6 @@ def tile_splitnn_pa_s_kernel(
         load_x(1, 2, 4)
         nc.sync.dma_start(out=noise_sb[:], in_=noise_std.rearrange("(p j) h -> p j h", j=J))
         load_weight(1)
-
         nc.gpsimd.dma_start(out=vec_rows[0:1, 2, :], in_=b2.rearrange("(o h) -> o h", o=1))
 
         xt_of, grouped_of, d_of, acc_of = {}, {}, {}, {}
@@ -256,15 +255,6 @@ def tile_splitnn_pa_s_kernel(
         nc.scalar.activation(out=abs_sb[:, 1, :], in_=a_sb[:, 1, :], func=ACT.Abs, accum_out=row_norm[:, 1 : 1 + 1])
         nc.scalar.activation(out=abs_sb[:, 2, :], in_=a_sb[:, 2, :], func=ACT.Abs, accum_out=row_norm[:, 2 : 2 + 1])
         nc.scalar.activation(out=abs_sb[:, 3, :], in_=a_sb[:, 3, :], func=ACT.Abs, accum_out=row_norm[:, 3 : 3 + 1])
-        bc2 = acc_pool.tile([P, 1, H], F32, tag="acc")
-        nc.tensor.matmul(
-            out=bc2[:].rearrange("p v h -> p (v h)"),
-            lhsT=ones[:],
-            rhs=vec_rows[:, 2:3, :].rearrange("p v h -> p (v h)"),
-            start=True,
-            stop=True,
-        )
-        nc.scalar.copy(out=b2_bc[:], in_=bc2[:, 0, :])
         transpose_unit(1, UNITS[1])
         regroup_unit(1, UNITS[1], nc.scalar.copy)
         transpose_unit(1, UNITS[2])
@@ -274,13 +264,22 @@ def tile_splitnn_pa_s_kernel(
         nc.vector.tensor_reduce(out=tile_ext[:, 0:1], in_=row_norm[:], axis=AX.X, op=ALU.max)
         nc.vector.tensor_reduce(out=tile_ext[:, 1:2], in_=row_norm[:], axis=AX.X, op=ALU.min, negate=True)
         nc.vector.tensor_tensor(out=a_kept[:, 0:4, :], in0=a_sb[:, 0:4, :], in1=keep_all[:, 0:4, :], op=ALU.mult)
+        transpose_unit(1, UNITS[3])
+        regroup_unit(1, UNITS[3], nc.scalar.copy)
         ext_ps = acc_pool.tile([P, 2, P], F32, tag="acc")
         for i in range(2):
             nc.tensor.transpose(ext_ps[:, i, :], tile_ext[:, i : i + 1].to_broadcast([P, P]), ident[:])
-        transpose_unit(1, UNITS[3])
-        regroup_unit(1, UNITS[3], nc.scalar.copy)
         transpose_unit(1, UNITS[4])
         regroup_unit(1, UNITS[4], nc.scalar.copy)
+        bc2 = acc_pool.tile([P, 1, H], F32, tag="acc")
+        nc.tensor.matmul(
+            out=bc2[:].rearrange("p v h -> p (v h)"),
+            lhsT=ones[:],
+            rhs=vec_rows[:, 2:3, :].rearrange("p v h -> p (v h)"),
+            start=True,
+            stop=True,
+        )
+        nc.scalar.copy(out=b2_bc[:], in_=bc2[:, 0, :])
         quantise_unit(1, UNITS[1])
         nc.vector.tensor_reduce(out=all_ext[:], in_=ext_ps[:], axis=AX.X, op=ALU.max)
         quantise_unit(1, UNITS[2])
@@ -294,12 +293,11 @@ def tile_splitnn_pa_s_kernel(
         )
         client2_mx(0, 2)
         quantise_unit(1, UNITS[3])
-        client2_add(0, 2)
-        noisy_rows(0, 2)
-        client2_mx(2, LAST)
         quantise_unit(1, UNITS[4])
-        noisy_rows(2, J)
+        client2_mx(2, LAST)
+        noisy_rows(0, J)
         client2_mx(LAST, J)
+        client2_add(0, 2)
         client2_add(2, LAST)
         finish_rows(0, 2)
         client2_add(LAST, J)

@@ -208,6 +208,13 @@ def tile_splitnn_pa_s_kernel(
             nc.vector.tensor_tensor(out=out_sb[:, j0:j1, :], in0=c_sb[:, j0:j1, :], in1=in1, op=ALU.min)
             nc.sync.dma_start(out=out_dram[:, j0:j1, :], in_=out_sb[:, j0:j1, :])
 
+        def warm_up():
+            warm_ps = acc_pool.tile([P, P], F32, tag="acc")
+            nc.tensor.matmul(out=warm_ps[:], lhsT=ident[:], rhs=ident[:], start=True, stop=True)
+
+        warm_up()
+        warm_up()
+        warm_up()
         transpose_unit(0, UNITS1[0])
         regroup_unit(0, UNITS1[0], nc.scalar.copy)
         transpose_unit(0, UNITS1[1])

from contextlib import ExitStack

import concourse.mybir as mybir
from concourse.masks import make_identity

F32 = mybir.dt.float32
BF16 = mybir.dt.bfloat16
I32 = mybir.dt.int32
U32 = mybir.dt.uint32
U8 = mybir.dt.uint8
FP8X4 = mybir.dt.float8_e4m3fn_x4
FP4X4 = mybir.dt.float4_e2m1fn_x4
ALU = mybir.AluOpType
ACT = mybir.ActivationFunctionType
AX = mybir.AxisListType

P = 128
PACK = 4
K_PASS = P * PACK
PAIRS = PACK // 2
B, F, H = 512, 1024, 128
J = B // P
G = F // K_PASS
LAST = J - 1
EPS = 4.0 / 30.0
P_KEEP = 0.95

UNITS = [(j, 0, G) for j in range(LAST)] + [(LAST, g, g + 1) for g in range(G)]
UNITS1 = [(0, g, g + 1) for g in range(G)] + UNITS[1:]

LAST_T = 0

FLOPS = 2 * 2 * B * F * H


def tile_splitnn_pa_s_kernel(
    tc, x1, x2, W1_words, W1_scales, b1, W2_words, W2_scales, b2, noise_std, rr_uniform, out
):
    nc = tc.nc
    x_dram = [x.rearrange("(p j) k -> p j k", j=J) for x in (x1, x2)]
    words_dram = (W1_words, W2_words)
    scales_dram = (W1_scales, W2_scales)
    out_dram = out.rearrange("(p j) h -> p j h", j=J)

    with ExitStack() as stack:
        const = stack.enter_context(tc.tile_pool(name="const", bufs=1))
        stage = stack.enter_context(tc.tile_pool(name="stage", bufs=6))
        xt_pool = stack.enter_context(tc.psum_pool(name="xt_pool", bufs=4))
        acc_pool = stack.enter_context(tc.psum_pool(name="acc_pool", bufs=4))
        stack.enter_context(tc.manual_schedule())

        x_sb0 = const.tile([P, J, F], BF16)
        x_sb1 = const.tile([P, J, F], BF16)
        x_sb = (x_sb0, x_sb1)
        w_words = const.tile([P, 2, G, 2 * H], U8, align_bytes=64)
        w_planes = const.tile([P, 2, G, H], U8, align_bytes=64)
        x_codes = const.tile([P, 2, J, G * P], U32, align_bytes=64)
        x_planes = const.tile([P, 2, J, G * P], U8, align_bytes=64)
        ident = const.tile([P, P], F32)
        ones = const.tile([P, P], BF16)
        vec_rows = const.tile([P, 3, H], BF16)
        b1_bc = const.tile([P, H], F32)
        b2_col = const.tile([P, 1], F32)
        d_t = const.tile([P, J, P], F32)
        b2_bc = const.tile([P, H], F32)
        keep_bc = const.tile([P, H], BF16)
        noise_sb = const.tile([P, J, H], BF16)
        noise_kept = const.tile([P, J, H], BF16)
        a_sb = const.tile([P, J, H], F32)
        a_kept = const.tile([P, J, H], F32)
        abs_sb = const.tile([P, J, H], F32)
        row_norm = const.tile([P, J], F32)
        tile_ext = const.tile([P, 2], F32)
        all_ext = const.tile([P, 2], F32)
        noise_mul = const.tile([P, 1], F32)
        c_sb = const.tile([P, J, H], F32)
        d_sb = const.tile([P, J, H], F32)
        out_sb = const.tile([P, J, H], F32)
        warm_in = const.tile([P, 1], F32)
        warm_out = const.tile([P, 1], F32)

        nc.vector.memset(vec_rows[:], 0.0)
        nc.vector.memset(ones[:], 1.0)
        nc.vector.memset(w_planes[:].rearrange("p c g h -> p (c g h)").bitcast(I32), 0)
        nc.vector.memset(warm_in[:], 0.0)
        make_identity(nc, ident[:])
        nc.scalar.activation(out=warm_out[:], in_=warm_in[:], func=ACT.Abs)

        def load_x(c, j0, j1):
            nc.sync.dma_start(out=x_sb[c][:, j0:j1, :], in_=x_dram[c][:, j0:j1, :])

        def load_vector(i, vec):
            nc.sync.dma_start(out=vec_rows[0:1, i, :], in_=vec.rearrange("(o h) -> o h", o=1))

        def load_weight(c):
            nc.sync.dma_start(
                out=w_words[:, c, :, :].bitcast(I32),
                in_=words_dram[c].bitcast(I32).rearrange("g p n -> p g n"),
            )
            for quad in range(4):
                nc.sync.dma_start(
                    out=w_planes[32 * quad : 32 * quad + 4, c, :, :].bitcast(I32),
                    in_=scales_dram[c].bitcast(I32)[:, 4 * quad : 4 * quad + 4, :].rearrange("g r n -> r g n"),
                )

        for g in range(G):
            k_cols = slice(g * K_PASS, (g + 1) * K_PASS)
            nc.sync.dma_start(out=x_sb[0][:, 0, k_cols], in_=x_dram[0][:, 0, k_cols])
        load_x(0, 1, 2)
        load_vector(0, b1)
        load_vector(1, rr_uniform)
        load_x(0, 2, 3)
        load_x(0, 3, 4)
        load_x(1, 0, 1)
        load_weight(0)
        load_x(1, 1, 2)
        load_x(1, 2, 4)
        nc.sync.dma_start(out=noise_sb[:], in_=noise_std.rearrange("(p j) h -> p j h", j=J))
        load_weight(1)
        nc.gpsimd.dma_start(out=vec_rows[0:1, 2, :], in_=b2.rearrange("(o h) -> o h", o=1))

        xt_of, grouped_of, d_of, acc_of = {}, {}, {}, {}

        def transpose_unit(c, unit):
            j, g0, g1 = unit
            n_pass = g1 - g0
            x_words = x_sb[c][:, j, :].bitcast(F32)
            xt = xt_pool.tile([P, n_pass * PAIRS, P], F32, tag="xt")
            for g in range(g0, g1):
                for u in range(PAIRS):
                    nc.tensor.transpose(
                        xt[:, PAIRS * (g - g0) + u, :],
                        x_words[:, 256 * g + u : 256 * (g + 1) : PAIRS],
                        ident[:],
                    )
            xt_of[(c, unit)] = xt

        def regroup_unit(c, unit, copy):
            j, g0, g1 = unit
            n_pass = g1 - g0
            grouped = stage.tile([P, n_pass * P * PACK], BF16, align_bytes=64, tag="grouped")
            copy(
                out=grouped[:].bitcast(F32).rearrange("p (g b u) -> p g b u", g=n_pass, u=PAIRS),
                in_=xt_of[(c, unit)][:].rearrange("p (g u) b -> p g b u", u=PAIRS),
            )
            grouped_of[(c, unit)] = grouped

        def quantise_unit(c, unit):
            j, g0, g1 = unit
            cols = slice(g0 * P, g1 * P)
            nc.vector.quantize_mx(
                out=x_codes[:, c, j, cols].bitcast(FP8X4),
                scales=x_planes[:, c, j, cols],
                in_=grouped_of[(c, unit)][:],
            )

        def project_tile(c, j, acc, transposed=False):
            for g in range(G):
                cols = slice(g * P, (g + 1) * P)
                x_side = (x_codes[:, c, j, cols].bitcast(FP8X4), x_planes[:, c, j, cols])
                w_side = (w_words[:, c, g, :].bitcast(FP4X4), w_planes[:, c, g, :])
                lhs, rhs = (w_side, x_side) if transposed else (x_side, w_side)
                nc.tensor.matmul_mx(
                    out=acc,
                    lhsT=lhs[0],
                    lhsT_scale=lhs[1],
                    rhs=rhs[0],
                    rhs_scale=rhs[1],
                    start=(g == 0),
                    stop=(g == G - 1),
                )

        def noisy_rows(j0, j1):
            nc.vector.scalar_tensor_tensor(
                out=c_sb[:, j0:j1, :].rearrange("p j h -> p (j h)"),
                in0=noise_kept[:, j0:j1, :].rearrange("p j h -> p (j h)"),
                scalar=noise_mul[:, 0:1],
                in1=a_kept[:, j0:j1, :].rearrange("p j h -> p (j h)"),
                op0=ALU.mult,
                op1=ALU.add,
            )

        def client2_mx(j0, j1):
            acc = acc_pool.tile([P, j1 - j0, H], F32, tag="acc")
            for j in range(j0, j1):
                project_tile(1, j, acc[:, j - j0, :])
            acc_of[j0] = acc

        def client2_add(j0, j1):
            b2_rows = b2_bc[:].unsqueeze(1).to_broadcast([P, j1 - j0, H])
            nc.vector.tensor_tensor(out=d_sb[:, j0:j1, :], in0=acc_of[j0][:], in1=b2_rows, op=ALU.add)

        def client2_product(j0, j1):
            acc = acc_pool.tile([P, j1 - j0, P], F32, tag="acc")
            for j in range(j0, j1):
                project_tile(1, j, acc[:, j - j0, :], transposed=True)
            nc.scalar.activation(out=d_t[:, j0:j1, :], in_=acc[:], func=ACT.Identity, bias=b2_col[:, 0:1])

        def client2_back(j0, j1):
            d_ps = xt_pool.tile([P, j1 - j0, H], F32, tag="xt")
            for j in range(j0, j1):
                nc.tensor.transpose(d_ps[:, j - j0, :], d_t[:, j, :], ident[:])
            d_of[j0] = d_ps

        def finish_rows(j0, j1):
            d = d_of[j0] if j0 in d_of else None
            in1 = d_sb[:, j0:j1, :] if d is None or j0 >= LAST_T else d[:]
            nc.vector.tensor_tensor(out=out_sb[:, j0:j1, :], in0=c_sb[:, j0:j1, :], in1=in1, op=ALU.min)
            nc.sync.dma_start(out=out_dram[:, j0:j1, :], in_=out_sb[:, j0:j1, :])

        def warm_up():
            warm_ps = acc_pool.tile([P, P], F32, tag="acc")
            nc.tensor.matmul(out=warm_ps[:], lhsT=ident[:], rhs=ident[:], start=True, stop=True)

        warm_up()
        warm_up()
        warm_up()
        transpose_unit(0, UNITS1[0])
        regroup_unit(0, UNITS1[0], nc.scalar.copy)
        transpose_unit(0, UNITS1[1])
        regroup_unit(0, UNITS1[1], nc.scalar.copy)
        quantise_unit(0, UNITS1[0])
        transpose_unit(0, UNITS1[2])
        regroup_unit(0, UNITS1[2], nc.scalar.copy)
        quantise_unit(0, UNITS1[1])
        bc1 = acc_pool.tile([P, 2, H], F32, tag="acc")
        nc.tensor.matmul(
            out=bc1[:].rearrange("p v h -> p (v h)"),
            lhsT=ones[:],
            rhs=vec_rows[:, 0:2, :].rearrange("p v h -> p (v h)"),
            start=True,
            stop=True,
        )
        nc.vector.tensor_copy(out=b1_bc[:], in_=bc1[:, 0, :])
        nc.vector.tensor_single_scalar(out=keep_bc[:], in_=bc1[:, 1, :], scalar=P_KEEP, op=ALU.is_lt)
        keep_all = keep_bc[:].unsqueeze(1).to_broadcast([P, J, H])
        transpose_unit(0, UNITS1[3])
        regroup_unit(0, UNITS1[3], nc.scalar.copy)
        quantise_unit(0, UNITS1[2])
        transpose_unit(0, UNITS1[4])
        regroup_unit(0, UNITS1[4], nc.scalar.copy)
        quantise_unit(0, UNITS1[3])
        transpose_unit(0, UNITS1[5])
        regroup_unit(0, UNITS1[5], nc.scalar.copy)
        quantise_unit(0, UNITS1[4])
        quantise_unit(0, UNITS1[5])
        transpose_unit(1, UNITS[0])
        regroup_unit(1, UNITS[0], nc.scalar.copy)
        acc1_0 = acc_pool.tile([P, H], F32, tag="acc")
        project_tile(0, 0, acc1_0[:])
        acc1_1 = acc_pool.tile([P, H], F32, tag="acc")
        project_tile(0, 1, acc1_1[:])
        nc.vector.tensor_tensor(out=a_sb[:, 0, :], in0=acc1_0[:], in1=b1_bc[:], op=ALU.add)
        nc.vector.tensor_tensor(out=a_sb[:, 1, :], in0=acc1_1[:], in1=b1_bc[:], op=ALU.add)
        acc1_2 = acc_pool.tile([P, H], F32, tag="acc")
        project_tile(0, 2, acc1_2[:])
        acc1_3 = acc_pool.tile([P, H], F32, tag="acc")
        project_tile(0, 3, acc1_3[:])
        nc.vector.tensor_tensor(out=a_sb[:, 2, :], in0=acc1_2[:], in1=b1_bc[:], op=ALU.add)
        nc.vector.tensor_tensor(out=a_sb[:, 3, :], in0=acc1_3[:], in1=b1_bc[:], op=ALU.add)
        nc.scalar.activation(out=abs_sb[:, 0, :], in_=a_sb[:, 0, :], func=ACT.Abs, accum_out=row_norm[:, 0 : 0 + 1])
        nc.scalar.activation(out=abs_sb[:, 1, :], in_=a_sb[:, 1, :], func=ACT.Abs, accum_out=row_norm[:, 1 : 1 + 1])
        nc.scalar.activation(out=abs_sb[:, 2, :], in_=a_sb[:, 2, :], func=ACT.Abs, accum_out=row_norm[:, 2 : 2 + 1])
        nc.scalar.activation(out=abs_sb[:, 3, :], in_=a_sb[:, 3, :], func=ACT.Abs, accum_out=row_norm[:, 3 : 3 + 1])
        transpose_unit(1, UNITS[1])
        regroup_unit(1, UNITS[1], nc.scalar.copy)
        transpose_unit(1, UNITS[2])
        regroup_unit(1, UNITS[2], nc.scalar.copy)
        quantise_unit(1, UNITS[0])
        nc.vector.tensor_tensor(out=noise_kept[:], in0=noise_sb[:], in1=keep_all, op=ALU.mult)
        nc.vector.tensor_reduce(out=tile_ext[:, 0:1], in_=row_norm[:], axis=AX.X, op=ALU.max)
        nc.vector.tensor_reduce(out=tile_ext[:, 1:2], in_=row_norm[:], axis=AX.X, op=ALU.min, negate=True)
        nc.vector.tensor_tensor(out=a_kept[:, 0:4, :], in0=a_sb[:, 0:4, :], in1=keep_all[:, 0:4, :], op=ALU.mult)
        transpose_unit(1, UNITS[3])
        regroup_unit(1, UNITS[3], nc.scalar.copy)
        ext_ps = acc_pool.tile([P, 2, P], F32, tag="acc")
        for i in range(2):
            nc.tensor.transpose(ext_ps[:, i, :], tile_ext[:, i : i + 1].to_broadcast([P, P]), ident[:])
        transpose_unit(1, UNITS[4])
        regroup_unit(1, UNITS[4], nc.scalar.copy)
        bc2 = acc_pool.tile([P, 1, H], F32, tag="acc")
        nc.tensor.matmul(
            out=bc2[:].rearrange("p v h -> p (v h)"),
            lhsT=ones[:],
            rhs=vec_rows[:, 2:3, :].rearrange("p v h -> p (v h)"),
            start=True,
            stop=True,
        )
        nc.scalar.copy(out=b2_bc[:], in_=bc2[:, 0, :])
        quantise_unit(1, UNITS[1])
        nc.vector.tensor_reduce(out=all_ext[:], in_=ext_ps[:], axis=AX.X, op=ALU.max)
        quantise_unit(1, UNITS[2])
        nc.vector.tensor_scalar(
            out=noise_mul[:],
            in0=all_ext[:, 0:1],
            scalar1=all_ext[:, 1:2],
            scalar2=1.0 / EPS,
            op0=ALU.add,
            op1=ALU.mult,
        )
        client2_mx(0, 2)
        quantise_unit(1, UNITS[3])
        quantise_unit(1, UNITS[4])
        client2_mx(2, LAST)
        noisy_rows(0, J)
        client2_mx(LAST, J)
        client2_add(0, 2)
        client2_add(2, LAST)
        finish_rows(0, 2)
        client2_add(LAST, J)
        finish_rows(2, LAST)
        finish_rows(LAST, J)
